import numpy as np
import ml_dtypes


def mxq(x, axis, fmt="e4m3"):
    dtype, down = {"e4m3": (ml_dtypes.float8_e4m3fn, 7), "e5m2": (ml_dtypes.float8_e5m2, 14)}[fmt]
    v = np.moveaxis(np.asarray(x, np.float32).astype(ml_dtypes.bfloat16).astype(np.float64), axis, -1)
    blocks = v.reshape(v.shape[:-1] + (-1, 32))
    amax = np.abs(blocks).max(-1, keepdims=True)
    byte = np.maximum(np.where(amax > 0, np.frexp(amax)[1] - 1 + 127, 0) - down, 1)
    scale = np.exp2(byte - 127.0)
    codes = (blocks / scale).astype(np.float32).astype(dtype).astype(np.float64)
    return np.moveaxis((codes * scale).reshape(v.shape), -1, axis)


WIDE = False


def mx_kscale(k):
    if not WIDE:
        return np.ones(k)
    levels = np.array([10, -10, 5, -5, 0])
    a = np.random.permutation(np.resize(levels, k // 512 * 4)).reshape(k // 512, 4)
    idx = np.arange(k)
    return np.exp2(a[idx // 512, idx % 128 // 32])


BF16 = ml_dtypes.bfloat16


def bf(x):
    return np.asarray(x, np.float32).astype(BF16)


def f64(x):
    return np.asarray(x).astype(np.float64)


B, S, D, H, QK, EXP, V, FI, LI, T = 8, 1024, 512, 2, 128, 128, 1024, 512, 768, 512
W = 2 * QK + 2 * EXP


def erf(a):
    c = np.clip(a, -6.0, 6.0)
    term = c.copy()
    tot = c.copy()
    for n in range(1, 120):
        term = term * (2.0 * c * c / (2 * n + 1))
        tot = tot + term
    r = 2.0 / np.sqrt(np.pi) * np.exp(-c * c) * tot
    return np.where(np.abs(a) > 6.0, np.sign(a), r)


def gelu(v):
    return 0.5 * v * (1.0 + erf(v / np.sqrt(2.0)))


def setup_inputs():
    s = mx_kscale(D)
    rows = np.concatenate([np.full(2 * QK, 1.5), np.ones(2 * EXP)])[:, None] / np.sqrt(D)
    x = np.random.standard_normal((B, S, D)) * (0.5 + np.random.random((B, S, 1))) + 0.3 * np.random.standard_normal((B, S, 1))
    return {"x": bf(x),
            "norm_w": bf((1.0 + 0.1 * np.random.standard_normal(D)) * s),
            "expand_w": bf(np.random.standard_normal((W, D)) * rows / s[None, :])}


def reference(x, norm_w, expand_w):
    x = f64(x)
    mu = x.mean(-1, keepdims=True)
    xc = x - mu
    var = (xc * xc).mean(-1, keepdims=True)
    xn = xc / np.sqrt(var + 1e-5) * f64(norm_w)
    proj = mxq(xn, 2, "e4m3") @ mxq(f64(expand_w), 1, "e4m3").T
    q = proj[..., :QK]
    k = proj[..., QK:2 * QK]
    lin = proj[..., 2 * QK:2 * QK + EXP]
    pre = proj[..., 2 * QK + EXP:]
    geglu = lin * gelu(pre)
    return q, k, geglu

@@ -1,0 +1,230 @@
+from contextlib import ExitStack
+
+import concourse.mybir as mybir
+from concourse.masks import make_identity
+
+F32 = mybir.dt.float32
+BF16 = mybir.dt.bfloat16
+U32 = mybir.dt.uint32
+U8 = mybir.dt.uint8
+FP8X4 = mybir.dt.float8_e4m3fn_x4
+ALU = mybir.AluOpType
+ACT = mybir.ActivationFunctionType
+
+P = 128
+PACK = 4
+D = P * PACK
+W_OUT = 512
+HEAD = 128
+TOKENS = 8 * 1024
+GROUP = 4
+N_GROUPS = TOKENS // (P * GROUP)
+EPS = 1e-5
+STATS_LEAD = 2
+
+FLOPS = 2 * TOKENS * D * W_OUT
+
+
+def tile_latentattentionblock_pa_t_kernel(tc, x, norm_w, expand_w, out_0, out_1, out_2):
+    nc = tc.nc
+    x_groups = x.flatten_outer_dims().rearrange("(g p j) k -> g p j k", p=P, j=GROUP)
+    q_groups = out_0.flatten_outer_dims().rearrange("(g p j) c -> g p j c", p=P, j=GROUP)
+    k_groups = out_1.flatten_outer_dims().rearrange("(g p j) c -> g p j c", p=P, j=GROUP)
+    geglu_groups = out_2.flatten_outer_dims().rearrange("(g p j) c -> g p j c", p=P, j=GROUP)
+
+    with ExitStack() as ctx:
+        consts = ctx.enter_context(tc.tile_pool(name="consts", bufs=1))
+        x_pool = ctx.enter_context(tc.tile_pool(name="x", bufs=N_GROUPS))
+        stat_pool = ctx.enter_context(tc.tile_pool(name="stats", bufs=STATS_LEAD + 2))
+        unread_pool = ctx.enter_context(tc.tile_pool(name="unread", bufs=4))
+        y_pool = ctx.enter_context(tc.tile_pool(name="y", bufs=2 * GROUP))
+        mx_pool = ctx.enter_context(tc.tile_pool(name="mx", bufs=2))
+        out_pool = ctx.enter_context(tc.tile_pool(name="outs", bufs=3))
+        turned_pool = ctx.enter_context(tc.psum_pool(name="turned", bufs=4))
+        proj_pool = ctx.enter_context(tc.psum_pool(name="proj", bufs=4))
+        ctx.enter_context(tc.manual_schedule())
+
+        eps_col = consts.tile([P, 1], F32)
+        nc.vector.memset(eps_col[:], EPS)
+        minus_half = consts.tile([P, GROUP], F32)
+        nc.vector.memset(minus_half[:], -0.5)
+        gain_rows = consts.tile([P, P], BF16)
+        nc.vector.memset(gain_rows[:], 0.0)
+        nc.scalar.dma_start(out=gain_rows[0:PACK, :], in_=norm_w.rearrange("(t p) -> t p", p=P))
+        table_warmer = consts.tile([P, 1], F32)
+        nc.scalar.activation(out=table_warmer[:], in_=eps_col[:], func=ACT.Gelu)
+        ident_f32 = consts.tile([P, P], F32)
+        make_identity(nc, ident_f32[:])
+        ident_bf16 = consts.tile([P, P], BF16)
+        make_identity(nc, ident_bf16[:])
+
+        x_tiles = {}
+
+        def load_x(g):
+            x_g = x_pool.tile([P, GROUP, D], BF16)
+            nc.sync.dma_start(out=x_g[:], in_=x_groups[g])
+            x_tiles[g] = x_g
+
+        load_x(0)
+        w_rows = consts.tile([P, W_OUT // P, D], BF16)
+        nc.sync.dma_start(out=w_rows[:], in_=expand_w.rearrange("(a p) k -> p a k", p=P))
+        for g in range(1, N_GROUPS):
+            load_x(g)
+
+        stats = {}
+
+        def statistics(g):
+            x_g = x_tiles[g]
+            half = GROUP // 2
+            var_eps = stat_pool.tile([P, 2, 8], F32)
+            bn = stat_pool.tile([P, half, 6], F32)
+            mean_var = stat_pool.tile([P, half, 2], F32)
+            for j in range(half):
+                nc.vector.bn_stats(out=bn[:, j, :], in_=x_g[:, j, :])
+            for j in range(half):
+                nc.vector.bn_aggr(out=mean_var[:, j, :], in_=bn[:, j, :])
+            negmean_v = stat_pool.tile([P, half], F32)
+            nc.vector.tensor_scalar_mul(out=negmean_v[:], in0=mean_var[:, :, 0], scalar1=-1.0)
+            nc.vector.tensor_scalar_add(out=var_eps[:, 0, 0:half], in0=mean_var[:, :, 1], scalar1=EPS)
+            negmean_s = stat_pool.tile([P, half], F32)
+            sum_sq = stat_pool.tile([P, half], F32)
+            for j in range(half):
+                unread = unread_pool.tile([P, D], BF16)
+                nc.scalar.activation(
+                    out=unread[:], in_=x_g[:, half + j, :], func=ACT.Identity,
+                    scale=-1.0 / D, accum_out=negmean_s[:, j : j + 1],
+                )
+            for j in range(half):
+                unread = unread_pool.tile([P, D], BF16)
+                nc.scalar.activation(
+                    out=unread[:], in_=x_g[:, half + j, :], func=ACT.Square,
+                    bias=negmean_s[:, j : j + 1], accum_out=sum_sq[:, j : j + 1],
+                )
+            nc.scalar.activation(
+                out=var_eps[:, 1, 0:half], in_=sum_sq[:], func=ACT.Identity,
+                scale=1.0 / D, bias=eps_col[:],
+            )
+            negmean = [negmean_v[:, 0:1], negmean_v[:, 1:2], negmean_s[:, 0:1], negmean_s[:, 1:2]]
+            stats[g] = (negmean, var_eps)
+
+        y_tiles = {}
+
+        def normalise(g):
+            negmean, var_eps = stats[g]
+            half = GROUP // 2
+            rstd = stat_pool.tile([P, GROUP], F32)
+            nc.gpsimd.tensor_tensor(
+                out=rstd[:].rearrange("p (h j) -> p h j", h=2),
+                in0=var_eps[:, :, 0:half],
+                in1=minus_half[:].rearrange("p (h j) -> p h j", h=2),
+                op=ALU.pow,
+            )
+            for j in range(GROUP):
+                y = y_pool.tile([P, D], F32)
+                nc.gpsimd.tensor_scalar(
+                    out=y[:], in0=x_tiles[g][:, j, :],
+                    scalar1=negmean[j], scalar2=rstd[:, j : j + 1], op0=ALU.add, op1=ALU.mult,
+                )
+                y_tiles[g, j] = y
+
+        turned_tiles = {}
+
+        def transpose(g):
+            for j in range(GROUP):
+                turned = turned_pool.tile([P, PACK, P], F32)
+                for t in range(PACK):
+                    nc.tensor.transpose(turned[:, t, :], y_tiles[g, j][:, t * P : (t + 1) * P], ident_f32[:])
+                turned_tiles[g, j] = turned
+
+        xn_tiles = {}
+
+        def regroup(g):
+            xn = mx_pool.tile([P, GROUP, P, PACK], BF16, align_bytes=64)
+            for j in range(GROUP):
+                nc.vector.tensor_tensor(
+                    out=xn[:, j, :, :],
+                    in0=turned_tiles[g, j][:].rearrange("p t r -> p r t"),
+                    in1=gain[:].unsqueeze(1).to_broadcast([P, P, PACK]),
+                    op=ALU.mult,
+                )
+            xn_tiles[g] = xn
+
+        mx_tiles = {}
+
+        def quantise(g):
+            codes = mx_pool.tile([P, GROUP * P], U32, align_bytes=64)
+            scales = mx_pool.tile([P, GROUP * P], U8, align_bytes=64)
+            nc.vector.quantize_mx(
+                out=codes[:].bitcast(FP8X4), scales=scales[:],
+                in_=xn_tiles[g][:].rearrange("p j r t -> p (j r t)"),
+            )
+            mx_tiles[g] = (codes, scales)
+
+        proj_tiles = {}
+
+        def project(g):
+            codes, scales = mx_tiles[g]
+            for j in range(GROUP):
+                proj = proj_pool.tile([P, W_OUT], F32)
+                nc.tensor.matmul_mx(
+                    out=proj[:],
+                    lhsT=codes[:, j * P : (j + 1) * P].bitcast(FP8X4),
+                    lhsT_scale=scales[:, j * P : (j + 1) * P],
+                    rhs=w_codes[:].bitcast(FP8X4),
+                    rhs_scale=w_scales[:],
+                    start=True, stop=True,
+                )
+                proj_tiles[g, j] = proj
+
+        def gate_and_store(g):
+            qk = out_pool.tile([P, 2, GROUP, HEAD], F32)
+            gelu_pre = out_pool.tile([P, GROUP, HEAD], F32)
+            geglu = out_pool.tile([P, GROUP, HEAD], F32)
+            for j in range(GROUP):
+                proj = proj_tiles[g, j]
+                nc.scalar.copy(
+                    out=qk[:, :, j, :], in_=proj[:, 0 : 2 * HEAD].rearrange("p (h c) -> p h c", h=2)
+                )
+                nc.scalar.activation(out=gelu_pre[:, j, :], in_=proj[:, 3 * HEAD : 4 * HEAD], func=ACT.Gelu)
+                nc.vector.tensor_tensor(
+                    out=geglu[:, j, :], in0=proj[:, 2 * HEAD : 3 * HEAD], in1=gelu_pre[:, j, :], op=ALU.mult
+                )
+            nc.sync.dma_start(out=q_groups[g], in_=qk[:, 0, :, :])
+            nc.sync.dma_start(out=k_groups[g], in_=qk[:, 1, :, :])
+            nc.sync.dma_start(out=geglu_groups[g], in_=geglu[:])
+
+        for g in range(STATS_LEAD):
+            statistics(g)
+
+        w_grouped = consts.tile([P, W_OUT, PACK], BF16, align_bytes=64)
+        for a in range(W_OUT // P):
+            w_turned = turned_pool.tile([P, PACK, P], BF16, tag="turned")
+            for t in range(PACK):
+                nc.tensor.transpose(w_turned[:, t, :], w_rows[:, a, t * P : (t + 1) * P], ident_bf16[:])
+            nc.vector.tensor_copy(
+                out=w_grouped[:, a * P : (a + 1) * P, :], in_=w_turned[:].rearrange("p t n -> p n t")
+            )
+        gain_turned = turned_pool.tile([P, P], BF16, tag="turned")
+        nc.tensor.transpose(gain_turned[:], gain_rows[:], ident_bf16[:])
+        gain = consts.tile([P, PACK], F32)
+        nc.vector.tensor_copy(out=gain[:], in_=gain_turned[:, 0:PACK])
+        w_codes = consts.tile([P, W_OUT], U32, align_bytes=64)
+        w_scales = consts.tile([P, W_OUT], U8, align_bytes=64)
+        nc.vector.quantize_mx(
+            out=w_codes[:].bitcast(FP8X4), scales=w_scales[:],
+            in_=w_grouped[:].rearrange("p n t -> p (n t)"),
+        )
+
+        for i in range(N_GROUPS + 2):
+            if 0 <= i - 1 < N_GROUPS:
+                regroup(i - 1)
+            if i < N_GROUPS:
+                normalise(i)
+                transpose(i)
+            if 0 <= i - 2:
+                gate_and_store(i - 2)
+            if 0 <= i - 1 < N_GROUPS:
+                quantise(i - 1)
+                project(i - 1)
+            if i + STATS_LEAD < N_GROUPS:
+                statistics(i + STATS_LEAD)

@@ -76,54 +76,48 @@ def tile_latentattentionblock_pa_t_kernel(tc, x, norm_w, expand_w, out_0, out_1,
         def statistics(g):
             x_g = x_tiles[g]
             half = GROUP // 2
-            var_eps = stat_pool.tile([P, 2, 8], F32)
             bn = stat_pool.tile([P, half, 6], F32)
             mean_var = stat_pool.tile([P, half, 2], F32)
             for j in range(half):
                 nc.vector.bn_stats(out=bn[:, j, :], in_=x_g[:, j, :])
             for j in range(half):
                 nc.vector.bn_aggr(out=mean_var[:, j, :], in_=bn[:, j, :])
-            negmean_v = stat_pool.tile([P, half], F32)
-            nc.vector.tensor_scalar_mul(out=negmean_v[:], in0=mean_var[:, :, 0], scalar1=-1.0)
-            nc.vector.tensor_scalar_add(out=var_eps[:, 0, 0:half], in0=mean_var[:, :, 1], scalar1=EPS)
-            negmean_s = stat_pool.tile([P, half], F32)
+            negmean = stat_pool.tile([P, GROUP], F32)
+            var_eps = stat_pool.tile([P, GROUP], F32)
             sum_sq = stat_pool.tile([P, half], F32)
             for j in range(half):
                 unread = unread_pool.tile([P, D], BF16)
                 nc.scalar.activation(
                     out=unread[:], in_=x_g[:, half + j, :], func=ACT.Identity,
-                    scale=-1.0 / D, accum_out=negmean_s[:, j : j + 1],
+                    scale=-1.0 / D, accum_out=negmean[:, half + j : half + j + 1],
                 )
             for j in range(half):
                 unread = unread_pool.tile([P, D], BF16)
                 nc.scalar.activation(
                     out=unread[:], in_=x_g[:, half + j, :], func=ACT.Square,
-                    bias=negmean_s[:, j : j + 1], accum_out=sum_sq[:, j : j + 1],
+                    bias=negmean[:, half + j : half + j + 1], accum_out=sum_sq[:, j : j + 1],
                 )
             nc.scalar.activation(
-                out=var_eps[:, 1, 0:half], in_=sum_sq[:], func=ACT.Identity,
+                out=var_eps[:, half:GROUP], in_=sum_sq[:], func=ACT.Identity,
                 scale=1.0 / D, bias=eps_col[:],
             )
-            negmean = [negmean_v[:, 0:1], negmean_v[:, 1:2], negmean_s[:, 0:1], negmean_s[:, 1:2]]
+            nc.scalar.activation(out=negmean[:, 0:half], in_=mean_var[:, :, 0], func=ACT.Identity, scale=-1.0)
+            nc.scalar.activation(
+                out=var_eps[:, 0:half], in_=mean_var[:, :, 1], func=ACT.Identity, bias=eps_col[:]
+            )
             stats[g] = (negmean, var_eps)
 
         y_tiles = {}
 
         def normalise(g):
             negmean, var_eps = stats[g]
-            half = GROUP // 2
             rstd = stat_pool.tile([P, GROUP], F32)
-            nc.gpsimd.tensor_tensor(
-                out=rstd[:].rearrange("p (h j) -> p h j", h=2),
-                in0=var_eps[:, :, 0:half],
-                in1=minus_half[:].rearrange("p (h j) -> p h j", h=2),
-                op=ALU.pow,
-            )
+            nc.gpsimd.tensor_tensor(out=rstd[:], in0=var_eps[:], in1=minus_half[:], op=ALU.pow)
             for j in range(GROUP):
                 y = y_pool.tile([P, D], F32)
                 nc.gpsimd.tensor_scalar(
                     out=y[:], in0=x_tiles[g][:, j, :],
-                    scalar1=negmean[j], scalar2=rstd[:, j : j + 1], op0=ALU.add, op1=ALU.mult,
+                    scalar1=negmean[:, j : j + 1], scalar2=rstd[:, j : j + 1], op0=ALU.add, op1=ALU.mult,
                 )
                 y_tiles[g, j] = y
 

@@ -20,6 +20,8 @@ TOKENS = 8 * 1024
 GROUP = 4
 N_GROUPS = TOKENS // (P * GROUP)
 EPS = 1e-5
+Q, K, LIN, PRE = 0, 1, 2, 3
+FILL_ORDER = (PRE, LIN, Q, K)
 STATS_LEAD = 2
 
 FLOPS = 2 * TOKENS * D * W_OUT
@@ -41,7 +43,7 @@ def tile_latentattentionblock_pa_t_kernel(tc, x, norm_w, expand_w, out_0, out_1,
         mx_pool = ctx.enter_context(tc.tile_pool(name="mx", bufs=2))
         out_pool = ctx.enter_context(tc.tile_pool(name="outs", bufs=3))
         turned_pool = ctx.enter_context(tc.psum_pool(name="turned", bufs=4))
-        proj_pool = ctx.enter_context(tc.psum_pool(name="proj", bufs=4))
+        proj_pool = ctx.enter_context(tc.psum_pool(name="proj", bufs=1))
         ctx.enter_context(tc.manual_schedule())
 
         eps_col = consts.tile([P, 1], F32)
@@ -158,34 +160,34 @@ def tile_latentattentionblock_pa_t_kernel(tc, x, norm_w, expand_w, out_0, out_1,
 
         def project(g):
             codes, scales = mx_tiles[g]
-            for j in range(GROUP):
-                proj = proj_pool.tile([P, W_OUT], F32)
-                nc.tensor.matmul_mx(
-                    out=proj[:],
-                    lhsT=codes[:, j * P : (j + 1) * P].bitcast(FP8X4),
-                    lhsT_scale=scales[:, j * P : (j + 1) * P],
-                    rhs=w_codes[:].bitcast(FP8X4),
-                    rhs_scale=w_scales[:],
-                    start=True, stop=True,
-                )
-                proj_tiles[g, j] = proj
+            banks = {}
+            for part in FILL_ORDER:
+                bank = proj_pool.tile([P, GROUP, HEAD], F32, tag="proj%d" % part)
+                for j in range(GROUP):
+                    nc.tensor.matmul_mx(
+                        out=bank[:, j, :],
+                        lhsT=codes[:, j * P : (j + 1) * P].bitcast(FP8X4),
+                        lhsT_scale=scales[:, j * P : (j + 1) * P],
+                        rhs=w_codes[:, part * HEAD : (part + 1) * HEAD].bitcast(FP8X4),
+                        rhs_scale=w_scales[:, part * HEAD : (part + 1) * HEAD],
+                        start=True, stop=True,
+                    )
+                banks[part] = bank
+            proj_tiles[g] = banks
 
         def gate_and_store(g):
-            qk = out_pool.tile([P, 2, GROUP, HEAD], F32)
+            banks = proj_tiles[g]
+            q_sb = out_pool.tile([P, GROUP, HEAD], F32)
+            k_sb = out_pool.tile([P, GROUP, HEAD], F32)
             gelu_pre = out_pool.tile([P, GROUP, HEAD], F32)
             geglu = out_pool.tile([P, GROUP, HEAD], F32)
-            for j in range(GROUP):
-                proj = proj_tiles[g, j]
-                nc.scalar.copy(
-                    out=qk[:, :, j, :], in_=proj[:, 0 : 2 * HEAD].rearrange("p (h c) -> p h c", h=2)
-                )
-                nc.scalar.activation(out=gelu_pre[:, j, :], in_=proj[:, 3 * HEAD : 4 * HEAD], func=ACT.Gelu)
-                nc.vector.tensor_tensor(
-                    out=geglu[:, j, :], in0=proj[:, 2 * HEAD : 3 * HEAD], in1=gelu_pre[:, j, :], op=ALU.mult
-                )
-            nc.sync.dma_start(out=q_groups[g], in_=qk[:, 0, :, :])
-            nc.sync.dma_start(out=k_groups[g], in_=qk[:, 1, :, :])
+            nc.scalar.activation(out=gelu_pre[:], in_=banks[PRE][:], func=ACT.Gelu)
+            nc.vector.tensor_tensor(out=geglu[:], in0=banks[LIN][:], in1=gelu_pre[:], op=ALU.mult)
             nc.sync.dma_start(out=geglu_groups[g], in_=geglu[:])
+            nc.scalar.copy(out=q_sb[:], in_=banks[Q][:])
+            nc.sync.dma_start(out=q_groups[g], in_=q_sb[:])
+            nc.scalar.copy(out=k_sb[:], in_=banks[K][:])
+            nc.sync.dma_start(out=k_groups[g], in_=k_sb[:])
 
         for g in range(STATS_LEAD):
             statistics(g)

@@ -22,6 +22,7 @@ N_GROUPS = TOKENS // (P * GROUP)
 EPS = 1e-5
 Q, K, LIN, PRE = 0, 1, 2, 3
 FILL_ORDER = (PRE, LIN, Q, K)
+SCALAR_SKIPS = 4
 STATS_LEAD = 2
 
 FLOPS = 2 * TOKENS * D * W_OUT
@@ -117,10 +118,20 @@ def tile_latentattentionblock_pa_t_kernel(tc, x, norm_w, expand_w, out_0, out_1,
             nc.gpsimd.tensor_tensor(out=rstd[:], in0=var_eps[:], in1=minus_half[:], op=ALU.pow)
             for j in range(GROUP):
                 y = y_pool.tile([P, D], F32)
-                nc.gpsimd.tensor_scalar(
-                    out=y[:], in0=x_tiles[g][:, j, :],
-                    scalar1=negmean[:, j : j + 1], scalar2=rstd[:, j : j + 1], op0=ALU.add, op1=ALU.mult,
-                )
+                if j == GROUP - 1 and g % SCALAR_SKIPS != 0:
+                    shift = stat_pool.tile([P, 1], F32)
+                    nc.scalar.activation(
+                        out=shift[:], in_=negmean[:, j : j + 1], func=ACT.Identity, scale=rstd[:, j : j + 1]
+                    )
+                    nc.scalar.activation(
+                        out=y[:], in_=x_tiles[g][:, j, :], func=ACT.Identity,
+                        scale=rstd[:, j : j + 1], bias=shift[:],
+                    )
+                else:
+                    nc.gpsimd.tensor_scalar(
+                        out=y[:], in0=x_tiles[g][:, j, :],
+                        scalar1=negmean[:, j : j + 1], scalar2=rstd[:, j : j + 1], op0=ALU.add, op1=ALU.mult,
+                    )
                 y_tiles[g, j] = y
 
         turned_tiles = {}
@@ -214,11 +225,11 @@ def tile_latentattentionblock_pa_t_kernel(tc, x, norm_w, expand_w, out_0, out_1,
         for i in range(N_GROUPS + 2):
             if 0 <= i - 1 < N_GROUPS:
                 regroup(i - 1)
+            if 0 <= i - 2:
+                gate_and_store(i - 2)
             if i < N_GROUPS:
                 normalise(i)
                 transpose(i)
-            if 0 <= i - 2:
-                gate_and_store(i - 2)
             if 0 <= i - 1 < N_GROUPS:
                 quantise(i - 1)
                 project(i - 1)

@@ -23,9 +23,19 @@ EPS = 1e-5
 Q, K, LIN, PRE = 0, 1, 2, 3
 FILL_ORDER = (PRE, LIN, Q, K)
 SCALAR_SKIPS = 4
-STATS_LEAD = 2
+BATCH = 2
+SINGLE_GROUPS = 2
+STATS_LEAD = 3
 
 FLOPS = 2 * TOKENS * D * W_OUT
+
+
+def folded_group(g):
+    return g >= SINGLE_GROUPS and g % 2 == 0
+
+
+def vector_share(g):
+    return 1 if folded_group(g) else 2
 
 
 def tile_latentattentionblock_pa_t_kernel(tc, x, norm_w, expand_w, out_0, out_1, out_2):
@@ -49,7 +59,7 @@ def tile_latentattentionblock_pa_t_kernel(tc, x, norm_w, expand_w, out_0, out_1,
 
         eps_col = consts.tile([P, 1], F32)
         nc.vector.memset(eps_col[:], EPS)
-        minus_half = consts.tile([P, GROUP], F32)
+        minus_half = consts.tile([P, BATCH, GROUP], F32)
         nc.vector.memset(minus_half[:], -0.5)
         gain_rows = consts.tile([P, P], BF16)
         nc.vector.memset(gain_rows[:], 0.0)
@@ -74,51 +84,98 @@ def tile_latentattentionblock_pa_t_kernel(tc, x, norm_w, expand_w, out_0, out_1,
         for g in range(1, N_GROUPS):
             load_x(g)
 
-        stats = {}
+        batch_tiles = {}
+
+        def batch_of(g):
+            if g < SINGLE_GROUPS:
+                return g, 1
+            first = g - (g - SINGLE_GROUPS) % BATCH
+            return first, min(BATCH, N_GROUPS - first)
+
+        def batch_tiles_of(g):
+            first, count = batch_of(g)
+            if first not in batch_tiles:
+                negmean = stat_pool.tile([P, BATCH, GROUP], F32)
+                var_eps = stat_pool.tile([P, BATCH, GROUP], F32)
+                batch_tiles[first] = (negmean, var_eps)
+            return batch_tiles[first]
+
+        def fold(g):
+            if not folded_group(g):
+                return
+            x_g = x_tiles[g]
+            negmean = batch_tiles_of(g)[0]
+            b = g - batch_of(g)[0]
+            share = vector_share(g)
+            quarters = turned_pool.tile([P, GROUP, P], F32, tag="turned")
+            for j in range(share, GROUP):
+                for t in range(PACK):
+                    nc.tensor.matmul(
+                        quarters[:, j, :], lhsT=ident_bf16[:], rhs=x_g[:, j, t * P : (t + 1) * P],
+                        start=(t == 0), stop=(t == PACK - 1),
+                    )
+            for j in range(share, GROUP):
+                unread = unread_pool.tile([P, D], BF16)
+                nc.scalar.activation(
+                    out=unread[:, 0:P], in_=quarters[:, j, :], func=ACT.Identity,
+                    scale=-1.0 / D, accum_out=negmean[:, b, j : j + 1],
+                )
 
         def statistics(g):
             x_g = x_tiles[g]
-            half = GROUP // 2
-            bn = stat_pool.tile([P, half, 6], F32)
-            mean_var = stat_pool.tile([P, half, 2], F32)
-            for j in range(half):
+            negmean, var_eps = batch_tiles_of(g)
+            b = g - batch_of(g)[0]
+            share = vector_share(g)
+            bn = stat_pool.tile([P, GROUP, 6], F32)
+            mean_var = stat_pool.tile([P, GROUP, 2], F32)
+            sum_sq = stat_pool.tile([P, GROUP], F32)
+            for j in range(share):
                 nc.vector.bn_stats(out=bn[:, j, :], in_=x_g[:, j, :])
-            for j in range(half):
+            for j in range(share):
                 nc.vector.bn_aggr(out=mean_var[:, j, :], in_=bn[:, j, :])
-            negmean = stat_pool.tile([P, GROUP], F32)
-            var_eps = stat_pool.tile([P, GROUP], F32)
-            sum_sq = stat_pool.tile([P, half], F32)
-            for j in range(half):
+            if not folded_group(g):
+                for j in range(share, GROUP):
+                    unread = unread_pool.tile([P, D], BF16)
+                    nc.scalar.activation(
+                        out=unread[:], in_=x_g[:, j, :], func=ACT.Identity,
+                        scale=-1.0 / D, accum_out=negmean[:, b, j : j + 1],
+                    )
+            for j in range(share, GROUP):
                 unread = unread_pool.tile([P, D], BF16)
                 nc.scalar.activation(
-                    out=unread[:], in_=x_g[:, half + j, :], func=ACT.Identity,
-                    scale=-1.0 / D, accum_out=negmean[:, half + j : half + j + 1],
-                )
-            for j in range(half):
-                unread = unread_pool.tile([P, D], BF16)
-                nc.scalar.activation(
-                    out=unread[:], in_=x_g[:, half + j, :], func=ACT.Square,
-                    bias=negmean[:, half + j : half + j + 1], accum_out=sum_sq[:, j : j + 1],
+                    out=unread[:], in_=x_g[:, j, :], func=ACT.Square,
+                    bias=negmean[:, b, j : j + 1], accum_out=sum_sq[:, j : j + 1],
                 )
             nc.scalar.activation(
-                out=var_eps[:, half:GROUP], in_=sum_sq[:], func=ACT.Identity,
+                out=var_eps[:, b, share:GROUP], in_=sum_sq[:, share:GROUP], func=ACT.Identity,
                 scale=1.0 / D, bias=eps_col[:],
             )
-            nc.scalar.activation(out=negmean[:, 0:half], in_=mean_var[:, :, 0], func=ACT.Identity, scale=-1.0)
             nc.scalar.activation(
-                out=var_eps[:, 0:half], in_=mean_var[:, :, 1], func=ACT.Identity, bias=eps_col[:]
+                out=negmean[:, b, 0:share], in_=mean_var[:, 0:share, 0], func=ACT.Identity, scale=-1.0
             )
-            stats[g] = (negmean, var_eps)
+            nc.scalar.activation(
+                out=var_eps[:, b, 0:share], in_=mean_var[:, 0:share, 1], func=ACT.Identity, bias=eps_col[:]
+            )
+
+        rstd_tiles = {}
 
         y_tiles = {}
 
         def normalise(g):
-            negmean, var_eps = stats[g]
-            rstd = stat_pool.tile([P, GROUP], F32)
-            nc.gpsimd.tensor_tensor(out=rstd[:], in0=var_eps[:], in1=minus_half[:], op=ALU.pow)
+            first, count = batch_of(g)
+            b = g - first
+            if b == 0:
+                rstd_all = stat_pool.tile([P, BATCH, GROUP], F32)
+                nc.gpsimd.tensor_tensor(
+                    out=rstd_all[:, 0:count, :], in0=batch_tiles[first][1][:, 0:count, :],
+                    in1=minus_half[:, 0:count, :], op=ALU.pow,
+                )
+                rstd_tiles[first] = rstd_all
+            negmean = batch_tiles[first][0][:, b, :]
+            rstd = rstd_tiles[first][:, b, :]
             for j in range(GROUP):
                 y = y_pool.tile([P, D], F32)
-                if j == GROUP - 1 and g % SCALAR_SKIPS != 0:
+                if j == GROUP - 1 and g % SCALAR_SKIPS == 1:
                     shift = stat_pool.tile([P, 1], F32)
                     nc.scalar.activation(
                         out=shift[:], in_=negmean[:, j : j + 1], func=ACT.Identity, scale=rstd[:, j : j + 1]
@@ -200,7 +257,7 @@ def tile_latentattentionblock_pa_t_kernel(tc, x, norm_w, expand_w, out_0, out_1,
             nc.scalar.copy(out=k_sb[:], in_=banks[K][:])
             nc.sync.dma_start(out=k_groups[g], in_=k_sb[:])
 
-        for g in range(STATS_LEAD):
+        for g in range(SINGLE_GROUPS):
             statistics(g)
 
         w_grouped = consts.tile([P, W_OUT, PACK], BF16, align_bytes=64)
@@ -221,12 +278,17 @@ def tile_latentattentionblock_pa_t_kernel(tc, x, norm_w, expand_w, out_0, out_1,
             out=w_codes[:].bitcast(FP8X4), scales=w_scales[:],
             in_=w_grouped[:].rearrange("p n t -> p (n t)"),
         )
+        for g in range(SINGLE_GROUPS, STATS_LEAD):
+            fold(g)
+            statistics(g)
 
         for i in range(N_GROUPS + 2):
             if 0 <= i - 1 < N_GROUPS:
                 regroup(i - 1)
             if 0 <= i - 2:
                 gate_and_store(i - 2)
+            if i + STATS_LEAD < N_GROUPS:
+                fold(i + STATS_LEAD)
             if i < N_GROUPS:
                 normalise(i)
                 transpose(i)

@@ -22,19 +22,21 @@ N_GROUPS = TOKENS // (P * GROUP)
 EPS = 1e-5
 Q, K, LIN, PRE = 0, 1, 2, 3
 FILL_ORDER = (PRE, LIN, Q, K)
-SCALAR_SKIPS = 4
 BATCH = 2
 SINGLE_GROUPS = 2
+FIRST_ORDER = (0, 3, 1, 2)
 STATS_LEAD = 3
 
 FLOPS = 2 * TOKENS * D * W_OUT
 
 
 def folded_group(g):
-    return g >= SINGLE_GROUPS and g % 2 == 0
+    return g % 2 == 1
 
 
 def vector_share(g):
+    if g == 0:
+        return 3
     return 1 if folded_group(g) else 2
 
 
@@ -59,7 +61,7 @@ def tile_latentattentionblock_pa_t_kernel(tc, x, norm_w, expand_w, out_0, out_1,
 
         eps_col = consts.tile([P, 1], F32)
         nc.vector.memset(eps_col[:], EPS)
-        minus_half = consts.tile([P, BATCH, GROUP], F32)
+        minus_half = consts.tile([P, BATCH * GROUP], F32)
         nc.vector.memset(minus_half[:], -0.5)
         gain_rows = consts.tile([P, P], BF16)
         nc.vector.memset(gain_rows[:], 0.0)
@@ -78,13 +80,17 @@ def tile_latentattentionblock_pa_t_kernel(tc, x, norm_w, expand_w, out_0, out_1,
             nc.sync.dma_start(out=x_g[:], in_=x_groups[g])
             x_tiles[g] = x_g
 
-        load_x(0)
+        x_first = x_pool.tile([P, GROUP, D], BF16, name="x_g")
+        for j in FIRST_ORDER:
+            nc.sync.dma_start(out=x_first[:, j, :], in_=x_groups[0][:, j, :])
+        x_tiles[0] = x_first
         w_rows = consts.tile([P, W_OUT // P, D], BF16)
         nc.sync.dma_start(out=w_rows[:], in_=expand_w.rearrange("(a p) k -> p a k", p=P))
         for g in range(1, N_GROUPS):
             load_x(g)
 
         batch_tiles = {}
+        column_of = {}
 
         def batch_of(g):
             if g < SINGLE_GROUPS:
@@ -95,9 +101,17 @@ def tile_latentattentionblock_pa_t_kernel(tc, x, norm_w, expand_w, out_0, out_1,
         def batch_tiles_of(g):
             first, count = batch_of(g)
             if first not in batch_tiles:
-                negmean = stat_pool.tile([P, BATCH, GROUP], F32)
-                var_eps = stat_pool.tile([P, BATCH, GROUP], F32)
-                batch_tiles[first] = (negmean, var_eps)
+                groups = range(first, first + count)
+                columns = [(h, j) for h in groups for j in range(vector_share(h))]
+                from_vector = len(columns)
+                columns.extend([(h, j) for h in groups for j in range(vector_share(h), GROUP)])
+                for c, tile_key in enumerate(columns):
+                    column_of[tile_key] = c
+                negmean = stat_pool.tile([P, BATCH * GROUP], F32)
+                var_eps = stat_pool.tile([P, BATCH * GROUP], F32)
+                sum_sq = stat_pool.tile([P, BATCH * GROUP], F32)
+                mean_var = stat_pool.tile([P, BATCH * GROUP, 2], F32)
+                batch_tiles[first] = (negmean, var_eps, sum_sq, mean_var, from_vector, len(columns))
             return batch_tiles[first]
 
         def fold(g):
@@ -105,7 +119,6 @@ def tile_latentattentionblock_pa_t_kernel(tc, x, norm_w, expand_w, out_0, out_1,
                 return
             x_g = x_tiles[g]
             negmean = batch_tiles_of(g)[0]
-            b = g - batch_of(g)[0]
             share = vector_share(g)
             quarters = turned_pool.tile([P, GROUP, P], F32, tag="turned")
             for j in range(share, GROUP):
@@ -115,47 +128,50 @@ def tile_latentattentionblock_pa_t_kernel(tc, x, norm_w, expand_w, out_0, out_1,
                         start=(t == 0), stop=(t == PACK - 1),
                     )
             for j in range(share, GROUP):
+                c = column_of[g, j]
                 unread = unread_pool.tile([P, D], BF16)
                 nc.scalar.activation(
                     out=unread[:, 0:P], in_=quarters[:, j, :], func=ACT.Identity,
-                    scale=-1.0 / D, accum_out=negmean[:, b, j : j + 1],
+                    scale=-1.0 / D, accum_out=negmean[:, c : c + 1],
                 )
 
         def statistics(g):
             x_g = x_tiles[g]
-            negmean, var_eps = batch_tiles_of(g)
-            b = g - batch_of(g)[0]
+            negmean, var_eps, sum_sq, mean_var, from_vector, n_columns = batch_tiles_of(g)
+            first, count = batch_of(g)
             share = vector_share(g)
             bn = stat_pool.tile([P, GROUP, 6], F32)
-            mean_var = stat_pool.tile([P, GROUP, 2], F32)
-            sum_sq = stat_pool.tile([P, GROUP], F32)
             for j in range(share):
                 nc.vector.bn_stats(out=bn[:, j, :], in_=x_g[:, j, :])
             for j in range(share):
-                nc.vector.bn_aggr(out=mean_var[:, j, :], in_=bn[:, j, :])
+                nc.vector.bn_aggr(out=mean_var[:, column_of[g, j], :], in_=bn[:, j, :])
             if not folded_group(g):
                 for j in range(share, GROUP):
+                    c = column_of[g, j]
                     unread = unread_pool.tile([P, D], BF16)
                     nc.scalar.activation(
                         out=unread[:], in_=x_g[:, j, :], func=ACT.Identity,
-                        scale=-1.0 / D, accum_out=negmean[:, b, j : j + 1],
+                        scale=-1.0 / D, accum_out=negmean[:, c : c + 1],
                     )
             for j in range(share, GROUP):
+                c = column_of[g, j]
                 unread = unread_pool.tile([P, D], BF16)
                 nc.scalar.activation(
                     out=unread[:], in_=x_g[:, j, :], func=ACT.Square,
-                    bias=negmean[:, b, j : j + 1], accum_out=sum_sq[:, j : j + 1],
+                    bias=negmean[:, c : c + 1], accum_out=sum_sq[:, c : c + 1],
                 )
-            nc.scalar.activation(
-                out=var_eps[:, b, share:GROUP], in_=sum_sq[:, share:GROUP], func=ACT.Identity,
-                scale=1.0 / D, bias=eps_col[:],
-            )
-            nc.scalar.activation(
-                out=negmean[:, b, 0:share], in_=mean_var[:, 0:share, 0], func=ACT.Identity, scale=-1.0
-            )
-            nc.scalar.activation(
-                out=var_eps[:, b, 0:share], in_=mean_var[:, 0:share, 1], func=ACT.Identity, bias=eps_col[:]
-            )
+            if g == first + count - 1:
+                nc.scalar.activation(
+                    out=var_eps[:, from_vector:n_columns], in_=sum_sq[:, from_vector:n_columns],
+                    func=ACT.Identity, scale=1.0 / D, bias=eps_col[:],
+                )
+                nc.scalar.activation(
+                    out=negmean[:, 0:from_vector], in_=mean_var[:, 0:from_vector, 0], func=ACT.Identity, scale=-1.0
+                )
+                nc.scalar.activation(
+                    out=var_eps[:, 0:from_vector], in_=mean_var[:, 0:from_vector, 1], func=ACT.Identity,
+                    bias=eps_col[:],
+                )
 
         rstd_tiles = {}
 
@@ -163,31 +179,34 @@ def tile_latentattentionblock_pa_t_kernel(tc, x, norm_w, expand_w, out_0, out_1,
 
         def normalise(g):
             first, count = batch_of(g)
-            b = g - first
-            if b == 0:
-                rstd_all = stat_pool.tile([P, BATCH, GROUP], F32)
+            n_columns = batch_tiles[first][5]
+            if g == first:
+                rstd_all = stat_pool.tile([P, BATCH * GROUP], F32)
                 nc.gpsimd.tensor_tensor(
-                    out=rstd_all[:, 0:count, :], in0=batch_tiles[first][1][:, 0:count, :],
-                    in1=minus_half[:, 0:count, :], op=ALU.pow,
+                    out=rstd_all[:, 0:n_columns], in0=batch_tiles[first][1][:, 0:n_columns],
+                    in1=minus_half[:, 0:n_columns], op=ALU.pow,
                 )
                 rstd_tiles[first] = rstd_all
-            negmean = batch_tiles[first][0][:, b, :]
-            rstd = rstd_tiles[first][:, b, :]
+            negmean_all = batch_tiles[first][0]
+            rstd_all = rstd_tiles[first]
             for j in range(GROUP):
                 y = y_pool.tile([P, D], F32)
-                if j == GROUP - 1 and g % SCALAR_SKIPS == 1:
+                c = column_of[g, j]
+                negmean = negmean_all[:, c : c + 1]
+                rstd = rstd_all[:, c : c + 1]
+                if j == GROUP - 1 and g > 0 and not folded_group(g):
                     shift = stat_pool.tile([P, 1], F32)
                     nc.scalar.activation(
-                        out=shift[:], in_=negmean[:, j : j + 1], func=ACT.Identity, scale=rstd[:, j : j + 1]
+                        out=shift[:], in_=negmean, func=ACT.Identity, scale=rstd
                     )
                     nc.scalar.activation(
                         out=y[:], in_=x_tiles[g][:, j, :], func=ACT.Identity,
-                        scale=rstd[:, j : j + 1], bias=shift[:],
+                        scale=rstd, bias=shift[:],
                     )
                 else:
                     nc.gpsimd.tensor_scalar(
                         out=y[:], in0=x_tiles[g][:, j, :],
-                        scalar1=negmean[:, j : j + 1], scalar2=rstd[:, j : j + 1], op0=ALU.add, op1=ALU.mult,
+                        scalar1=negmean, scalar2=rstd, op0=ALU.add, op1=ALU.mult,
                     )
                 y_tiles[g, j] = y
 
@@ -202,36 +221,43 @@ def tile_latentattentionblock_pa_t_kernel(tc, x, norm_w, expand_w, out_0, out_1,
 
         xn_tiles = {}
 
-        def regroup(g):
-            xn = mx_pool.tile([P, GROUP, P, PACK], BF16, align_bytes=64)
-            for j in range(GROUP):
+        def regroup(g, lo=0, hi=GROUP):
+            if lo == 0:
+                xn_tiles[g] = mx_pool.tile([P, GROUP, P, PACK], BF16, align_bytes=64, name="xn")
+            xn = xn_tiles[g]
+            for j in range(lo, hi):
                 nc.vector.tensor_tensor(
                     out=xn[:, j, :, :],
                     in0=turned_tiles[g, j][:].rearrange("p t r -> p r t"),
                     in1=gain[:].unsqueeze(1).to_broadcast([P, P, PACK]),
                     op=ALU.mult,
                 )
-            xn_tiles[g] = xn
 
         mx_tiles = {}
 
-        def quantise(g):
-            codes = mx_pool.tile([P, GROUP * P], U32, align_bytes=64)
-            scales = mx_pool.tile([P, GROUP * P], U8, align_bytes=64)
+        def quantise(g, lo=0, hi=GROUP):
+            if lo == 0:
+                codes = mx_pool.tile([P, GROUP * P], U32, align_bytes=64)
+                scales = mx_pool.tile([P, GROUP * P], U8, align_bytes=64)
+                mx_tiles[g] = (codes, scales)
+            codes, scales = mx_tiles[g]
             nc.vector.quantize_mx(
-                out=codes[:].bitcast(FP8X4), scales=scales[:],
-                in_=xn_tiles[g][:].rearrange("p j r t -> p (j r t)"),
+                out=codes[:, lo * P : hi * P].bitcast(FP8X4), scales=scales[:, lo * P : hi * P],
+                in_=xn_tiles[g][:, lo:hi, :, :].rearrange("p j r t -> p (j r t)"),
             )
-            mx_tiles[g] = (codes, scales)
 
         proj_tiles = {}
 
-        def project(g):
+        def project(g, lo=0, hi=GROUP):
             codes, scales = mx_tiles[g]
-            banks = {}
+            if lo == 0:
+                proj_tiles[g] = {}
+            banks = proj_tiles[g]
             for part in FILL_ORDER:
-                bank = proj_pool.tile([P, GROUP, HEAD], F32, tag="proj%d" % part)
-                for j in range(GROUP):
+                if lo == 0:
+                    banks[part] = proj_pool.tile([P, GROUP, HEAD], F32, tag="proj%d" % part, name="bank")
+                bank = banks[part]
+                for j in range(lo, hi):
                     nc.tensor.matmul_mx(
                         out=bank[:, j, :],
                         lhsT=codes[:, j * P : (j + 1) * P].bitcast(FP8X4),
@@ -240,25 +266,29 @@ def tile_latentattentionblock_pa_t_kernel(tc, x, norm_w, expand_w, out_0, out_1,
                         rhs_scale=w_scales[:, part * HEAD : (part + 1) * HEAD],
                         start=True, stop=True,
                     )
-                banks[part] = bank
-            proj_tiles[g] = banks
 
-        def gate_and_store(g):
+        out_tiles = {}
+
+        def gate_and_store(g, lo=0, hi=GROUP):
             banks = proj_tiles[g]
-            q_sb = out_pool.tile([P, GROUP, HEAD], F32)
-            k_sb = out_pool.tile([P, GROUP, HEAD], F32)
-            gelu_pre = out_pool.tile([P, GROUP, HEAD], F32)
-            geglu = out_pool.tile([P, GROUP, HEAD], F32)
-            nc.scalar.activation(out=gelu_pre[:], in_=banks[PRE][:], func=ACT.Gelu)
-            nc.vector.tensor_tensor(out=geglu[:], in0=banks[LIN][:], in1=gelu_pre[:], op=ALU.mult)
-            nc.sync.dma_start(out=geglu_groups[g], in_=geglu[:])
-            nc.scalar.copy(out=q_sb[:], in_=banks[Q][:])
-            nc.sync.dma_start(out=q_groups[g], in_=q_sb[:])
-            nc.scalar.copy(out=k_sb[:], in_=banks[K][:])
-            nc.sync.dma_start(out=k_groups[g], in_=k_sb[:])
+            if lo == 0:
+                q_sb = out_pool.tile([P, GROUP, HEAD], F32)
+                k_sb = out_pool.tile([P, GROUP, HEAD], F32)
+                gelu_pre = out_pool.tile([P, GROUP, HEAD], F32)
+                geglu = out_pool.tile([P, GROUP, HEAD], F32)
+                out_tiles[g] = (q_sb, k_sb, gelu_pre, geglu)
+            q_sb, k_sb, gelu_pre, geglu = out_tiles[g]
+            nc.scalar.activation(out=gelu_pre[:, lo:hi, :], in_=banks[PRE][:, lo:hi, :], func=ACT.Gelu)
+            nc.vector.tensor_tensor(
+                out=geglu[:, lo:hi, :], in0=banks[LIN][:, lo:hi, :], in1=gelu_pre[:, lo:hi, :], op=ALU.mult
+            )
+            nc.sync.dma_start(out=geglu_groups[g][:, lo:hi, :], in_=geglu[:, lo:hi, :])
+            nc.scalar.copy(out=q_sb[:, lo:hi, :], in_=banks[Q][:, lo:hi, :])
+            nc.sync.dma_start(out=q_groups[g][:, lo:hi, :], in_=q_sb[:, lo:hi, :])
+            nc.scalar.copy(out=k_sb[:, lo:hi, :], in_=banks[K][:, lo:hi, :])
+            nc.sync.dma_start(out=k_groups[g][:, lo:hi, :], in_=k_sb[:, lo:hi, :])
 
-        for g in range(SINGLE_GROUPS):
-            statistics(g)
+        statistics(0)
 
         w_grouped = consts.tile([P, W_OUT, PACK], BF16, align_bytes=64)
         for a in range(W_OUT // P):
@@ -278,11 +308,11 @@ def tile_latentattentionblock_pa_t_kernel(tc, x, norm_w, expand_w, out_0, out_1,
             out=w_codes[:].bitcast(FP8X4), scales=w_scales[:],
             in_=w_grouped[:].rearrange("p n t -> p (n t)"),
         )
-        for g in range(SINGLE_GROUPS, STATS_LEAD):
+        for g in range(1, STATS_LEAD):
             fold(g)
             statistics(g)
 
-        for i in range(N_GROUPS + 2):
+        for i in range(N_GROUPS):
             if 0 <= i - 1 < N_GROUPS:
                 regroup(i - 1)
             if 0 <= i - 2:
@@ -297,3 +327,15 @@ def tile_latentattentionblock_pa_t_kernel(tc, x, norm_w, expand_w, out_0, out_1,
                 project(i - 1)
             if i + STATS_LEAD < N_GROUPS:
                 statistics(i + STATS_LEAD)
+
+        last = N_GROUPS - 1
+        half = GROUP // 2
+        regroup(last, 0, half)
+        gate_and_store(last - 1)
+        quantise(last, 0, half)
+        project(last, 0, half)
+        regroup(last, half, GROUP)
+        gate_and_store(last, 0, half)
+        quantise(last, half, GROUP)
+        project(last, half, GROUP)
+        gate_and_store(last, half, GROUP)

@@ -25,6 +25,7 @@ FILL_ORDER = (PRE, LIN, Q, K)
 BATCH = 2
 SINGLE_GROUPS = 2
 FIRST_ORDER = (0, 3, 1, 2)
+FOLD = 64
 STATS_LEAD = 3
 
 FLOPS = 2 * TOKENS * D * W_OUT
@@ -120,18 +121,18 @@ def tile_latentattentionblock_pa_t_kernel(tc, x, norm_w, expand_w, out_0, out_1,
             x_g = x_tiles[g]
             negmean = batch_tiles_of(g)[0]
             share = vector_share(g)
-            quarters = turned_pool.tile([P, GROUP, P], F32, tag="turned")
+            quarters = turned_pool.tile([P, GROUP, FOLD], F32, tag="turned")
             for j in range(share, GROUP):
-                for t in range(PACK):
+                for t in range(D // FOLD):
                     nc.tensor.matmul(
-                        quarters[:, j, :], lhsT=ident_bf16[:], rhs=x_g[:, j, t * P : (t + 1) * P],
-                        start=(t == 0), stop=(t == PACK - 1),
+                        quarters[:, j, :], lhsT=ident_bf16[:], rhs=x_g[:, j, t * FOLD : (t + 1) * FOLD],
+                        start=(t == 0), stop=(t == D // FOLD - 1),
                     )
             for j in range(share, GROUP):
                 c = column_of[g, j]
                 unread = unread_pool.tile([P, D], BF16)
                 nc.scalar.activation(
-                    out=unread[:, 0:P], in_=quarters[:, j, :], func=ACT.Identity,
+                    out=unread[:, 0:FOLD], in_=quarters[:, j, :], func=ACT.Identity,
                     scale=-1.0 / D, accum_out=negmean[:, c : c + 1],
                 )
 

from contextlib import ExitStack

import concourse.mybir as mybir
from concourse.masks import make_identity

F32 = mybir.dt.float32
BF16 = mybir.dt.bfloat16
U32 = mybir.dt.uint32
U8 = mybir.dt.uint8
FP8X4 = mybir.dt.float8_e4m3fn_x4
ALU = mybir.AluOpType
ACT = mybir.ActivationFunctionType

P = 128
PACK = 4
D = P * PACK
W_OUT = 512
HEAD = 128
TOKENS = 8 * 1024
GROUP = 4
N_GROUPS = TOKENS // (P * GROUP)
EPS = 1e-5
Q, K, LIN, PRE = 0, 1, 2, 3
FILL_ORDER = (PRE, LIN, Q, K)
BATCH = 2
SINGLE_GROUPS = 2
FIRST_ORDER = (0, 3, 1, 2)
FOLD = 64
STATS_LEAD = 3

FLOPS = 2 * TOKENS * D * W_OUT


def folded_group(g):
    return g % 2 == 1


def vector_share(g):
    if g == 0:
        return 3
    return 1 if folded_group(g) else 2


def tile_latentattentionblock_pa_t_kernel(tc, x, norm_w, expand_w, out_0, out_1, out_2):
    nc = tc.nc
    x_groups = x.flatten_outer_dims().rearrange("(g p j) k -> g p j k", p=P, j=GROUP)
    q_groups = out_0.flatten_outer_dims().rearrange("(g p j) c -> g p j c", p=P, j=GROUP)
    k_groups = out_1.flatten_outer_dims().rearrange("(g p j) c -> g p j c", p=P, j=GROUP)
    geglu_groups = out_2.flatten_outer_dims().rearrange("(g p j) c -> g p j c", p=P, j=GROUP)

    with ExitStack() as ctx:
        consts = ctx.enter_context(tc.tile_pool(name="consts", bufs=1))
        x_pool = ctx.enter_context(tc.tile_pool(name="x", bufs=N_GROUPS))
        stat_pool = ctx.enter_context(tc.tile_pool(name="stats", bufs=STATS_LEAD + 2))
        unread_pool = ctx.enter_context(tc.tile_pool(name="unread", bufs=4))
        y_pool = ctx.enter_context(tc.tile_pool(name="y", bufs=2 * GROUP))
        mx_pool = ctx.enter_context(tc.tile_pool(name="mx", bufs=2))
        out_pool = ctx.enter_context(tc.tile_pool(name="outs", bufs=3))
        turned_pool = ctx.enter_context(tc.psum_pool(name="turned", bufs=4))
        proj_pool = ctx.enter_context(tc.psum_pool(name="proj", bufs=1))
        ctx.enter_context(tc.manual_schedule())

        eps_col = consts.tile([P, 1], F32)
        nc.vector.memset(eps_col[:], EPS)
        minus_half = consts.tile([P, BATCH * GROUP], F32)
        nc.vector.memset(minus_half[:], -0.5)
        gain_rows = consts.tile([P, P], BF16)
        nc.vector.memset(gain_rows[:], 0.0)
        nc.scalar.dma_start(out=gain_rows[0:PACK, :], in_=norm_w.rearrange("(t p) -> t p", p=P))
        table_warmer = consts.tile([P, 1], F32)
        nc.scalar.activation(out=table_warmer[:], in_=eps_col[:], func=ACT.Gelu)
        ident_f32 = consts.tile([P, P], F32)
        make_identity(nc, ident_f32[:])
        ident_bf16 = consts.tile([P, P], BF16)
        make_identity(nc, ident_bf16[:])

        x_tiles = {}

        def load_x(g):
            x_g = x_pool.tile([P, GROUP, D], BF16)
            nc.sync.dma_start(out=x_g[:], in_=x_groups[g])
            x_tiles[g] = x_g

        x_first = x_pool.tile([P, GROUP, D], BF16, name="x_g")
        for j in FIRST_ORDER:
            nc.sync.dma_start(out=x_first[:, j, :], in_=x_groups[0][:, j, :])
        x_tiles[0] = x_first
        w_rows = consts.tile([P, W_OUT // P, D], BF16)
        nc.sync.dma_start(out=w_rows[:], in_=expand_w.rearrange("(a p) k -> p a k", p=P))
        for g in range(1, N_GROUPS):
            load_x(g)

        batch_tiles = {}
        column_of = {}

        def batch_of(g):
            if g < SINGLE_GROUPS:
                return g, 1
            first = g - (g - SINGLE_GROUPS) % BATCH
            return first, min(BATCH, N_GROUPS - first)

        def batch_tiles_of(g):
            first, count = batch_of(g)
            if first not in batch_tiles:
                groups = range(first, first + count)
                columns = [(h, j) for h in groups for j in range(vector_share(h))]
                from_vector = len(columns)
                columns.extend([(h, j) for h in groups for j in range(vector_share(h), GROUP)])
                for c, tile_key in enumerate(columns):
                    column_of[tile_key] = c
                negmean = stat_pool.tile([P, BATCH * GROUP], F32)
                var_eps = stat_pool.tile([P, BATCH * GROUP], F32)
                sum_sq = stat_pool.tile([P, BATCH * GROUP], F32)
                mean_var = stat_pool.tile([P, BATCH * GROUP, 2], F32)
                batch_tiles[first] = (negmean, var_eps, sum_sq, mean_var, from_vector, len(columns))
            return batch_tiles[first]

        def fold(g):
            if not folded_group(g):
                return
            x_g = x_tiles[g]
            negmean = batch_tiles_of(g)[0]
            share = vector_share(g)
            quarters = turned_pool.tile([P, GROUP, FOLD], F32, tag="turned")
            for j in range(share, GROUP):
                for t in range(D // FOLD):
                    nc.tensor.matmul(
                        quarters[:, j, :], lhsT=ident_bf16[:], rhs=x_g[:, j, t * FOLD : (t + 1) * FOLD],
                        start=(t == 0), stop=(t == D // FOLD - 1),
                    )
            for j in range(share, GROUP):
                c = column_of[g, j]
                unread = unread_pool.tile([P, D], BF16)
                nc.scalar.activation(
                    out=unread[:, 0:FOLD], in_=quarters[:, j, :], func=ACT.Identity,
                    scale=-1.0 / D, accum_out=negmean[:, c : c + 1],
                )

        def statistics(g):
            x_g = x_tiles[g]
            negmean, var_eps, sum_sq, mean_var, from_vector, n_columns = batch_tiles_of(g)
            first, count = batch_of(g)
            share = vector_share(g)
            bn = stat_pool.tile([P, GROUP, 6], F32)
            for j in range(share):
                nc.vector.bn_stats(out=bn[:, j, :], in_=x_g[:, j, :])
            for j in range(share):
                nc.vector.bn_aggr(out=mean_var[:, column_of[g, j], :], in_=bn[:, j, :])
            if not folded_group(g):
                for j in range(share, GROUP):
                    c = column_of[g, j]
                    unread = unread_pool.tile([P, D], BF16)
                    nc.scalar.activation(
                        out=unread[:], in_=x_g[:, j, :], func=ACT.Identity,
                        scale=-1.0 / D, accum_out=negmean[:, c : c + 1],
                    )
            for j in range(share, GROUP):
                c = column_of[g, j]
                unread = unread_pool.tile([P, D], BF16)
                nc.scalar.activation(
                    out=unread[:], in_=x_g[:, j, :], func=ACT.Square,
                    bias=negmean[:, c : c + 1], accum_out=sum_sq[:, c : c + 1],
                )
            if g == first + count - 1:
                nc.scalar.activation(
                    out=var_eps[:, from_vector:n_columns], in_=sum_sq[:, from_vector:n_columns],
                    func=ACT.Identity, scale=1.0 / D, bias=eps_col[:],
                )
                nc.scalar.activation(
                    out=negmean[:, 0:from_vector], in_=mean_var[:, 0:from_vector, 0], func=ACT.Identity, scale=-1.0
                )
                nc.scalar.activation(
                    out=var_eps[:, 0:from_vector], in_=mean_var[:, 0:from_vector, 1], func=ACT.Identity,
                    bias=eps_col[:],
                )

        rstd_tiles = {}

        y_tiles = {}

        def normalise(g):
            first, count = batch_of(g)
            n_columns = batch_tiles[first][5]
            if g == first:
                rstd_all = stat_pool.tile([P, BATCH * GROUP], F32)
                nc.gpsimd.tensor_tensor(
                    out=rstd_all[:, 0:n_columns], in0=batch_tiles[first][1][:, 0:n_columns],
                    in1=minus_half[:, 0:n_columns], op=ALU.pow,
                )
                rstd_tiles[first] = rstd_all
            negmean_all = batch_tiles[first][0]
            rstd_all = rstd_tiles[first]
            for j in range(GROUP):
                y = y_pool.tile([P, D], F32)
                c = column_of[g, j]
                negmean = negmean_all[:, c : c + 1]
                rstd = rstd_all[:, c : c + 1]
                if j == GROUP - 1 and g > 0 and not folded_group(g):
                    shift = stat_pool.tile([P, 1], F32)
                    nc.scalar.activation(
                        out=shift[:], in_=negmean, func=ACT.Identity, scale=rstd
                    )
                    nc.scalar.activation(
                        out=y[:], in_=x_tiles[g][:, j, :], func=ACT.Identity,
                        scale=rstd, bias=shift[:],
                    )
                else:
                    nc.gpsimd.tensor_scalar(
                        out=y[:], in0=x_tiles[g][:, j, :],
                        scalar1=negmean, scalar2=rstd, op0=ALU.add, op1=ALU.mult,
                    )
                y_tiles[g, j] = y

        turned_tiles = {}

        def transpose(g):
            for j in range(GROUP):
                turned = turned_pool.tile([P, PACK, P], F32)
                for t in range(PACK):
                    nc.tensor.transpose(turned[:, t, :], y_tiles[g, j][:, t * P : (t + 1) * P], ident_f32[:])
                turned_tiles[g, j] = turned

        xn_tiles = {}

        def regroup(g, lo=0, hi=GROUP):
            if lo == 0:
                xn_tiles[g] = mx_pool.tile([P, GROUP, P, PACK], BF16, align_bytes=64, name="xn")
            xn = xn_tiles[g]
            for j in range(lo, hi):
                nc.vector.tensor_tensor(
                    out=xn[:, j, :, :],
                    in0=turned_tiles[g, j][:].rearrange("p t r -> p r t"),
                    in1=gain[:].unsqueeze(1).to_broadcast([P, P, PACK]),
                    op=ALU.mult,
                )

        mx_tiles = {}

        def quantise(g, lo=0, hi=GROUP):
            if lo == 0:
                codes = mx_pool.tile([P, GROUP * P], U32, align_bytes=64)
                scales = mx_pool.tile([P, GROUP * P], U8, align_bytes=64)
                mx_tiles[g] = (codes, scales)
            codes, scales = mx_tiles[g]
            nc.vector.quantize_mx(
                out=codes[:, lo * P : hi * P].bitcast(FP8X4), scales=scales[:, lo * P : hi * P],
                in_=xn_tiles[g][:, lo:hi, :, :].rearrange("p j r t -> p (j r t)"),
            )

        proj_tiles = {}

        def project(g, lo=0, hi=GROUP):
            codes, scales = mx_tiles[g]
            if lo == 0:
                proj_tiles[g] = {}
            banks = proj_tiles[g]
            for part in FILL_ORDER:
                if lo == 0:
                    banks[part] = proj_pool.tile([P, GROUP, HEAD], F32, tag="proj%d" % part, name="bank")
                bank = banks[part]
                for j in range(lo, hi):
                    nc.tensor.matmul_mx(
                        out=bank[:, j, :],
                        lhsT=codes[:, j * P : (j + 1) * P].bitcast(FP8X4),
                        lhsT_scale=scales[:, j * P : (j + 1) * P],
                        rhs=w_codes[:, part * HEAD : (part + 1) * HEAD].bitcast(FP8X4),
                        rhs_scale=w_scales[:, part * HEAD : (part + 1) * HEAD],
                        start=True, stop=True,
                    )

        out_tiles = {}

        def gate_and_store(g, lo=0, hi=GROUP):
            banks = proj_tiles[g]
            if lo == 0:
                q_sb = out_pool.tile([P, GROUP, HEAD], F32)
                k_sb = out_pool.tile([P, GROUP, HEAD], F32)
                gelu_pre = out_pool.tile([P, GROUP, HEAD], F32)
                geglu = out_pool.tile([P, GROUP, HEAD], F32)
                out_tiles[g] = (q_sb, k_sb, gelu_pre, geglu)
            q_sb, k_sb, gelu_pre, geglu = out_tiles[g]
            nc.scalar.activation(out=gelu_pre[:, lo:hi, :], in_=banks[PRE][:, lo:hi, :], func=ACT.Gelu)
            nc.vector.tensor_tensor(
                out=geglu[:, lo:hi, :], in0=banks[LIN][:, lo:hi, :], in1=gelu_pre[:, lo:hi, :], op=ALU.mult
            )
            nc.sync.dma_start(out=geglu_groups[g][:, lo:hi, :], in_=geglu[:, lo:hi, :])
            nc.scalar.copy(out=q_sb[:, lo:hi, :], in_=banks[Q][:, lo:hi, :])
            nc.sync.dma_start(out=q_groups[g][:, lo:hi, :], in_=q_sb[:, lo:hi, :])
            nc.scalar.copy(out=k_sb[:, lo:hi, :], in_=banks[K][:, lo:hi, :])
            nc.sync.dma_start(out=k_groups[g][:, lo:hi, :], in_=k_sb[:, lo:hi, :])

        statistics(0)

        w_grouped = consts.tile([P, W_OUT, PACK], BF16, align_bytes=64)
        for a in range(W_OUT // P):
            w_turned = turned_pool.tile([P, PACK, P], BF16, tag="turned")
            for t in range(PACK):
                nc.tensor.transpose(w_turned[:, t, :], w_rows[:, a, t * P : (t + 1) * P], ident_bf16[:])
            nc.vector.tensor_copy(
                out=w_grouped[:, a * P : (a + 1) * P, :], in_=w_turned[:].rearrange("p t n -> p n t")
            )
        gain_turned = turned_pool.tile([P, P], BF16, tag="turned")
        nc.tensor.transpose(gain_turned[:], gain_rows[:], ident_bf16[:])
        gain = consts.tile([P, PACK], F32)
        nc.vector.tensor_copy(out=gain[:], in_=gain_turned[:, 0:PACK])
        w_codes = consts.tile([P, W_OUT], U32, align_bytes=64)
        w_scales = consts.tile([P, W_OUT], U8, align_bytes=64)
        nc.vector.quantize_mx(
            out=w_codes[:].bitcast(FP8X4), scales=w_scales[:],
            in_=w_grouped[:].rearrange("p n t -> p (n t)"),
        )
        for g in range(1, STATS_LEAD):
            fold(g)
            statistics(g)

        for i in range(N_GROUPS):
            if 0 <= i - 1 < N_GROUPS:
                regroup(i - 1)
            if 0 <= i - 2:
                gate_and_store(i - 2)
            if i + STATS_LEAD < N_GROUPS:
                fold(i + STATS_LEAD)
            if i < N_GROUPS:
                normalise(i)
                transpose(i)
            if 0 <= i - 1 < N_GROUPS:
                quantise(i - 1)
                project(i - 1)
            if i + STATS_LEAD < N_GROUPS:
                statistics(i + STATS_LEAD)

        last = N_GROUPS - 1
        half = GROUP // 2
        regroup(last, 0, half)
        gate_and_store(last - 1)
        quantise(last, 0, half)
        project(last, 0, half)
        regroup(last, half, GROUP)
        gate_and_store(last, 0, half)
        quantise(last, half, GROUP)
        project(last, half, GROUP)
        gate_and_store(last, half, GROUP)
